import numpy as np
import ml_dtypes


def mxq(x, axis, fmt="e4m3"):
    dtype, down = {"e4m3": (ml_dtypes.float8_e4m3fn, 7), "e5m2": (ml_dtypes.float8_e5m2, 14)}[fmt]
    v = np.moveaxis(np.asarray(x, np.float32).astype(ml_dtypes.bfloat16).astype(np.float64), axis, -1)
    blocks = v.reshape(v.shape[:-1] + (-1, 32))
    amax = np.abs(blocks).max(-1, keepdims=True)
    byte = np.maximum(np.where(amax > 0, np.frexp(amax)[1] - 1 + 127, 0) - down, 1)
    scale = np.exp2(byte - 127.0)
    codes = (blocks / scale).astype(np.float32).astype(dtype).astype(np.float64)
    return np.moveaxis((codes * scale).reshape(v.shape), -1, axis)


WIDE = False


def mx_kscale(k):
    if not WIDE:
        return np.ones(k)
    levels = np.array([10, -10, 5, -5, 0])
    if k % 512:
        return np.exp2(np.random.permutation(np.resize(levels, k // 32))).repeat(32)
    a = np.empty((k // 512, 16))
    for p in range(k // 512):
        a[p, :8] = np.random.permutation(np.resize(levels, 8))
        for g in range(8):
            far = levels[np.abs(levels - a[p, g]) >= 10]
            a[p, g + 8] = far[np.random.randint(len(far))]
    return np.exp2(a.ravel()).repeat(32)


BF16 = ml_dtypes.bfloat16


def bf(x):
    return np.asarray(x, np.float32).astype(BF16)


def f64(x):
    return np.asarray(x).astype(np.float64)


B, C, HD, F, G, O = 128, 8, 8, 1024, 512, 128
N = C * HD


def setup_inputs():
    s, t = mx_kscale(F), mx_kscale(G)
    return {
        "x": bf(np.random.standard_normal((B, C, HD, F)) * s),
        "W1g": bf(np.random.standard_normal((G, F)) * 0.7 * np.sqrt(N / F) / s * t[:, None]),
        "b1g": bf(np.random.standard_normal(G) * 0.2 * t),
        "W2g": bf(np.random.standard_normal((O, G)) * 1.5 / np.sqrt(G) / t),
        "b2g": bf(np.random.standard_normal(O) * 0.2),
    }


def reference(x, W1g, b1g, W2g, b2g):
    xn = f64(x).reshape(B * N, F)
    y = mxq(xn, 1, "e4m3") @ mxq(f64(W1g), 1, "e4m3").T
    m1 = np.maximum(y.reshape(B, N, G).sum(1) / N + f64(b1g), 0.0)
    m2 = np.maximum((mxq(m1, 1, "e4m3") @ mxq(f64(W2g), 1, "e4m3").T) + f64(b2g), 0.0)
    return np.broadcast_to(m2[:, None, :], (B, N, O)).copy()

@@ -1,0 +1,312 @@
+from contextlib import ExitStack
+
+import concourse.mybir as mybir
+from concourse.masks import make_identity
+
+F32 = mybir.dt.float32
+BF16 = mybir.dt.bfloat16
+U32 = mybir.dt.uint32
+U8 = mybir.dt.uint8
+FP8X4 = mybir.dt.float8_e4m3fn_x4
+ALU = mybir.AluOpType
+AX = mybir.AxisListType
+
+P = 128
+NODES = 64
+FEAT = 1024
+HID = 512
+OUTF = 128
+SLOTS = 4
+UNITS = 16
+UNIT_COLS = SLOTS * FEAT
+UNIT_WORDS = UNIT_COLS // 4
+PASSES = 8
+
+FLOPS = 2 * 8192 * FEAT * HID + 2 * 128 * HID * OUTF
+
+GROUP_UNITS = (8, 4, 2, 2)
+NARROW_GROUPS = (2, 3)
+HEAD_STEPS = ((4, 4),) * 6
+RUN_SLOTS = 2
+SECOND_LAG = (16, 16, 12, 0)
+TAIL_STEP = 4
+SMALL_LOADS_AFTER = 6
+SMALL_STEP = 7
+VECTOR_HEAD_SLOTS = 16
+
+
+def plan_steps():
+    steps = list(HEAD_STEPS)
+    slots = sum([a for a, b in steps])
+    passes = sum([b for a, b in steps])
+    while slots < UNITS * SLOTS:
+        a = min(RUN_SLOTS, UNITS * SLOTS - slots)
+        steps.append((a, 2 * a))
+        slots += a
+        passes += 2 * a
+    while passes < UNITS * PASSES:
+        steps.append((0, TAIL_STEP))
+        passes += TAIL_STEP
+    return steps
+
+
+def plan_passes():
+    order = []
+    unit0 = 0
+    for grp_i, n_units in enumerate(GROUP_UNITS):
+        units = range(unit0, unit0 + n_units)
+        if grp_i == len(GROUP_UNITS) - 1:
+            order.extend([(grp_i, i, j, g) for j in range(SLOTS) for i in units for g in range(2)])
+        else:
+            order.extend([(grp_i, i, j, g) for i in units for j in range(SLOTS) for g in range(2)])
+        unit0 += n_units
+    return order
+
+
+def tile_gcn_pa_t_kernel(tc, x, W1g, b1g, W2g, b2g, out):
+    nc = tc.nc
+    ctx = ExitStack()
+    with ctx:
+        const = ctx.enter_context(tc.tile_pool(name="const", bufs=1))
+        xpool = ctx.enter_context(tc.tile_pool(name="xpool", bufs=UNITS))
+        gpool = ctx.enter_context(tc.tile_pool(name="gpool", bufs=3))
+        cpool = ctx.enter_context(tc.tile_pool(name="cpool", bufs=5))
+        epool = ctx.enter_context(tc.tile_pool(name="epool", bufs=2))
+        tpool = ctx.enter_context(tc.psum_pool(name="tpool", bufs=4))
+        apool = ctx.enter_context(tc.psum_pool(name="apool", bufs=1))
+        ctx.enter_context(tc.manual_schedule())
+
+        unit_group = []
+        unit_pos = []
+        x_views = []
+        o_views = []
+        x_rows = x.flatten_outer_dims()
+        o_rows = out.flatten_outer_dims()
+        row0 = 0
+        for grp_i, n_units in enumerate(GROUP_UNITS):
+            rows = n_units * SLOTS * P
+            x_views.append(x_rows[row0 : row0 + rows, :].rearrange("(q s) f -> q (s f)", q=P))
+            o_views.append(o_rows[row0 : row0 + rows, :].rearrange("(q s) o -> q s o", q=P))
+            row0 += rows
+            for c in range(n_units):
+                unit_group.append(grp_i)
+                unit_pos.append(c)
+
+        ident = const.tile([P, P], F32)
+        make_identity(nc, ident[:])
+
+        xt = []
+        for i in range(UNITS):
+            x_sb = xpool.tile([P, UNIT_COLS], BF16, name="x_sb")
+            xt.append(x_sb)
+        w1raw = const.tile([P, UNIT_COLS], BF16)
+        w1v = W1g.rearrange("(p j) k -> p (j k)", j=SLOTS)
+        w2raw = const.tile([P, HID], BF16)
+        b1raw = const.tile([P, SLOTS], BF16)
+        b2raw = const.tile([P, OUTF], BF16)
+
+        def load_x(i, pieces):
+            c0 = unit_pos[i] * UNIT_COLS
+            w = UNIT_COLS // pieces
+            for s in range(pieces):
+                nc.sync.dma_start(
+                    out=xt[i][:, s * w : (s + 1) * w],
+                    in_=x_views[unit_group[i]][:, c0 + s * w : c0 + (s + 1) * w],
+                )
+
+        load_x(0, SLOTS)
+        for j in range(SLOTS):
+            nc.sync.dma_start(out=w1raw[:, j * FEAT : (j + 1) * FEAT], in_=w1v[:, j * FEAT : (j + 1) * FEAT])
+        for i in range(1, UNITS):
+            load_x(i, 1)
+            if i == SMALL_LOADS_AFTER:
+                nc.sync.dma_start(out=w2raw[:], in_=W2g)
+                nc.sync.dma_start(out=b1raw[:], in_=b1g.rearrange("(p j) -> p j", j=SLOTS))
+                nc.sync.dma_start(out=b2raw[:], in_=b2g.partition_broadcast(P))
+
+        w1grp = const.tile([P, UNIT_COLS], BF16, align_bytes=64)
+        w1codes = const.tile([P, UNIT_WORDS], U32, align_bytes=64)
+        w1scales = const.tile([P, UNIT_WORDS], U8, align_bytes=64)
+        w2grp = const.tile([P, HID], BF16, align_bytes=64)
+        w2codes = const.tile([P, OUTF], U32, align_bytes=64)
+        w2scales = const.tile([P, OUTF], U8, align_bytes=64)
+        b1f = const.tile([P, SLOTS], F32)
+        b2f = const.tile([P, OUTF], F32)
+
+        grouped = {}
+        quantised = {}
+        accs = {}
+        hidden_parts = {}
+        hidden_codes = {}
+
+        def transposes(src_f32, s):
+            bank = tpool.tile([P, 512], F32, name="bank")
+            for v in range(4):
+                nc.tensor.transpose(
+                    bank[:, v * P : (v + 1) * P],
+                    src_f32[:, s * 512 + (v // 2) * 256 + v % 2 : s * 512 + (v // 2 + 1) * 256 : 2],
+                    ident[:],
+                )
+            return bank
+
+        def copy_slot(slot, bank):
+            i, s = divmod(slot, SLOTS)
+            if s == 0:
+                grp = gpool.tile([P, UNIT_COLS], BF16, name="grp", align_bytes=64)
+                grouped[i] = grp
+            dst = grouped[i][:].bitcast(F32).rearrange("p (g h q u) -> p g h q u", g=2, h=SLOTS, q=P, u=2)
+            src = bank[:].rearrange("p (g u q) -> p g q u", g=2, u=2, q=P)
+            if slot < VECTOR_HEAD_SLOTS and slot % 2 == 1:
+                nc.vector.tensor_copy(out=dst[:, :, s, :, :], in_=src)
+            else:
+                nc.scalar.copy(out=dst[:, :, s, :, :], in_=src)
+
+        def quant_x(i):
+            codes = cpool.tile([P, UNIT_WORDS], U32, name="codes", align_bytes=64)
+            scales = cpool.tile([P, UNIT_WORDS], U8, name="scales", align_bytes=64)
+            nc.vector.quantize_mx(out=codes[:].bitcast(FP8X4), scales=scales[:], in_=grouped[i][:])
+            quantised[i] = (codes, scales)
+
+        def prep_w1():
+            src = w1raw[:].bitcast(F32)
+            grp_v = w1grp[:].bitcast(F32).rearrange("p (j g m u) -> p j g m u", j=SLOTS, g=2, m=P, u=2)
+            for j in range(SLOTS):
+                bank = transposes(src, j)
+                nc.scalar.copy(out=grp_v[:, j, :, :, :], in_=bank[:].rearrange("p (g u m) -> p g m u", g=2, u=2, m=P))
+                nc.vector.quantize_mx(
+                    out=w1codes[:, j * 256 : (j + 1) * 256].bitcast(FP8X4),
+                    scales=w1scales[:, j * 256 : (j + 1) * 256],
+                    in_=w1grp[:, j * FEAT : (j + 1) * FEAT],
+                )
+
+        def prep_small():
+            src = w2raw[:].bitcast(F32).rearrange("p (w u) -> p u w", u=2)
+            bank = tpool.tile([P, 512], F32, name="bank")
+            for u in range(2):
+                nc.tensor.transpose(bank[:, u * P : (u + 1) * P], src[:, u, :], ident[:])
+            nc.vector.tensor_copy(
+                out=w2grp[:].bitcast(F32).rearrange("p (o u) -> p o u", u=2),
+                in_=bank[:, 0 : 2 * P].rearrange("p (u o) -> p o u", u=2),
+            )
+            nc.vector.tensor_copy(out=b1f[:], in_=b1raw[:])
+            nc.vector.tensor_copy(out=b2f[:], in_=b2raw[:])
+            nc.vector.quantize_mx(out=w2codes[:].bitcast(FP8X4), scales=w2scales[:], in_=w2grp[:])
+
+        def one_pass(grp_i, i, j, g):
+            first = unit_pos[i] == 0 and g == 0
+            last = unit_pos[i] == GROUP_UNITS[grp_i] - 1 and g == 1
+            if first:
+                acc = apool.tile([P, 512], F32, name="acc%d" % j)
+                accs[j] = acc
+            codes, scales = quantised[i]
+            w = (j * 2 + g) * P
+            parts = 2 if grp_i in NARROW_GROUPS else 1
+            width = 512 // parts
+            for part in range(parts):
+                c0 = g * 512 + part * width
+                nc.tensor.matmul_mx(
+                    out=accs[j][:, 0:width],
+                    lhsT=w1codes[:, w : w + P].bitcast(FP8X4),
+                    lhsT_scale=w1scales[:, w : w + P],
+                    rhs=codes[:, c0 : c0 + width].bitcast(FP8X4),
+                    rhs_scale=scales[:, c0 : c0 + width],
+                    start=(first and part == 0),
+                    stop=(last and part == parts - 1),
+                )
+            return last
+
+        def node_sum(grp_i, j):
+            nb = 8 * GROUP_UNITS[grp_i]
+            parts = 2 if grp_i in NARROW_GROUPS else 1
+            if j == 0:
+                sums = epool.tile([P, 256], F32, name="sums")
+                m1pre = epool.tile([P, HID], BF16, name="m1pre")
+                hidden_parts[grp_i] = (sums, m1pre)
+            sums, m1pre = hidden_parts[grp_i]
+            nc.vector.tensor_reduce(
+                out=sums[:, j * nb : (j + 1) * nb],
+                in_=accs[j][:, 0 : 512 // parts].rearrange("p (h b l) -> p b h l", h=SLOTS // parts, b=nb, l=P // nb),
+                axis=AX.XY,
+                op=ALU.add,
+            )
+            nc.vector.tensor_scalar(
+                out=m1pre[:].rearrange("p (b r j) -> p b r j", b=nb, r=P // nb, j=SLOTS)[:, :, :, j],
+                in0=sums[:, j * nb : (j + 1) * nb].unsqueeze(2).to_broadcast([P, nb, P // nb]),
+                scalar1=1.0 / NODES,
+                scalar2=b1f[:, j : j + 1],
+                op0=ALU.mult,
+                op1=ALU.add,
+            )
+
+        def hidden(grp_i):
+            m1pre = hidden_parts[grp_i][1]
+            m1 = epool.tile([P, HID], BF16, name="m1", align_bytes=64)
+            nc.vector.tensor_scalar_max(out=m1[:], in0=m1pre[:], scalar1=0.0)
+            m1codes = epool.tile([P, P], U32, name="m1codes", align_bytes=64)
+            m1scales = epool.tile([P, P], U8, name="m1scales", align_bytes=64)
+            nc.vector.quantize_mx(out=m1codes[:].bitcast(FP8X4), scales=m1scales[:], in_=m1[:])
+            hidden_codes[grp_i] = (m1codes, m1scales)
+
+        def second(grp_i):
+            m1codes, m1scales = hidden_codes[grp_i]
+            bank = tpool.tile([P, 512], F32, name="bank")
+            nc.tensor.matmul_mx(
+                out=bank[:, 0:OUTF],
+                lhsT=m1codes[:].bitcast(FP8X4),
+                lhsT_scale=m1scales[:],
+                rhs=w2codes[:].bitcast(FP8X4),
+                rhs_scale=w2scales[:],
+                start=True,
+                stop=True,
+            )
+            pre2 = epool.tile([P, OUTF], F32, name="pre2")
+            nc.vector.tensor_tensor(out=pre2[:], in0=bank[:, 0:OUTF], in1=b2f[:], op=ALU.add)
+            m2 = epool.tile([P, OUTF], F32, name="m2")
+            nc.vector.tensor_scalar_max(out=m2[:], in0=pre2[:], scalar1=0.0)
+            n_rep = SLOTS * GROUP_UNITS[grp_i]
+            nc.sync.dma_start(out=o_views[grp_i], in_=m2[:].unsqueeze(1).to_broadcast([P, n_rep, OUTF]))
+
+        pass_order = plan_passes()
+        n_slots = 0
+        n_passes = 0
+        n_quant = 0
+        to_hide = []
+        to_second = []
+        for step, (run_slots, run_passes) in enumerate(plan_steps()):
+            while n_quant < UNITS and SLOTS * (n_quant + 1) <= n_slots:
+                quant_x(n_quant)
+                n_quant += 1
+            for grp_i in to_hide:
+                hidden(grp_i)
+            to_hide = []
+            banks = []
+            for k in range(run_slots):
+                i, s = divmod(n_slots + k, SLOTS)
+                banks.append(transposes(xt[i][:].bitcast(F32), s))
+            for k in range(run_slots):
+                copy_slot(n_slots + k, banks[k])
+            n_slots += run_slots
+            if step == 0:
+                quant_x(0)
+                n_quant = 1
+                prep_w1()
+            if step == SMALL_STEP:
+                prep_small()
+            for k in range(run_passes):
+                grp_i, i, j, g = pass_order[n_passes]
+                closes = one_pass(grp_i, i, j, g)
+                n_passes += 1
+                if closes:
+                    node_sum(grp_i, j)
+                    if j == SLOTS - 1:
+                        to_hide.append(grp_i)
+                        to_second.append((grp_i, n_passes))
+            if n_passes == UNITS * PASSES:
+                for grp_i in to_hide:
+                    hidden(grp_i)
+                to_hide = []
+            while to_second and (
+                n_passes - to_second[0][1] >= SECOND_LAG[to_second[0][0]] or n_passes == UNITS * PASSES
+            ):
+                second(to_second[0][0])
+                to_second = to_second[1:]

@@ -20,47 +20,12 @@ SLOTS = 4
 UNITS = 16
 UNIT_COLS = SLOTS * FEAT
 UNIT_WORDS = UNIT_COLS // 4
-PASSES = 8
 
 FLOPS = 2 * 8192 * FEAT * HID + 2 * 128 * HID * OUTF
 
 GROUP_UNITS = (8, 4, 2, 2)
-NARROW_GROUPS = (2, 3)
-HEAD_STEPS = ((4, 4),) * 6
-RUN_SLOTS = 2
-SECOND_LAG = (16, 16, 12, 0)
-TAIL_STEP = 4
-SMALL_LOADS_AFTER = 6
-SMALL_STEP = 7
-VECTOR_HEAD_SLOTS = 16
-
-
-def plan_steps():
-    steps = list(HEAD_STEPS)
-    slots = sum([a for a, b in steps])
-    passes = sum([b for a, b in steps])
-    while slots < UNITS * SLOTS:
-        a = min(RUN_SLOTS, UNITS * SLOTS - slots)
-        steps.append((a, 2 * a))
-        slots += a
-        passes += 2 * a
-    while passes < UNITS * PASSES:
-        steps.append((0, TAIL_STEP))
-        passes += TAIL_STEP
-    return steps
-
-
-def plan_passes():
-    order = []
-    unit0 = 0
-    for grp_i, n_units in enumerate(GROUP_UNITS):
-        units = range(unit0, unit0 + n_units)
-        if grp_i == len(GROUP_UNITS) - 1:
-            order.extend([(grp_i, i, j, g) for j in range(SLOTS) for i in units for g in range(2)])
-        else:
-            order.extend([(grp_i, i, j, g) for i in units for j in range(SLOTS) for g in range(2)])
-        unit0 += n_units
-    return order
+SMALL_LOADS_AFTER = 4
+SMALL_STEP = 3
 
 
 def tile_gcn_pa_t_kernel(tc, x, W1g, b1g, W2g, b2g, out):
@@ -68,12 +33,13 @@ def tile_gcn_pa_t_kernel(tc, x, W1g, b1g, W2g, b2g, out):
     ctx = ExitStack()
     with ctx:
         const = ctx.enter_context(tc.tile_pool(name="const", bufs=1))
-        xpool = ctx.enter_context(tc.tile_pool(name="xpool", bufs=UNITS))
+        xpool = ctx.enter_context(tc.tile_pool(name="xpool", bufs=12))
+        ppool = ctx.enter_context(tc.tile_pool(name="ppool", bufs=3))
         gpool = ctx.enter_context(tc.tile_pool(name="gpool", bufs=3))
-        cpool = ctx.enter_context(tc.tile_pool(name="cpool", bufs=5))
+        cpool = ctx.enter_context(tc.tile_pool(name="cpool", bufs=4))
         epool = ctx.enter_context(tc.tile_pool(name="epool", bufs=2))
-        tpool = ctx.enter_context(tc.psum_pool(name="tpool", bufs=4))
-        apool = ctx.enter_context(tc.psum_pool(name="apool", bufs=1))
+        tpool = ctx.enter_context(tc.psum_pool(name="tpool", bufs=6))
+        apool = ctx.enter_context(tc.psum_pool(name="apool", bufs=2))
         ctx.enter_context(tc.manual_schedule())
 
         unit_group = []
@@ -95,29 +61,30 @@ def tile_gcn_pa_t_kernel(tc, x, W1g, b1g, W2g, b2g, out):
         ident = const.tile([P, P], F32)
         make_identity(nc, ident[:])
 
-        xt = []
-        for i in range(UNITS):
-            x_sb = xpool.tile([P, UNIT_COLS], BF16, name="x_sb")
-            xt.append(x_sb)
         w1raw = const.tile([P, UNIT_COLS], BF16)
         w1v = W1g.rearrange("(p j) k -> p (j k)", j=SLOTS)
         w2raw = const.tile([P, HID], BF16)
         b1raw = const.tile([P, SLOTS], BF16)
         b2raw = const.tile([P, OUTF], BF16)
 
+        xt = []
+
         def load_x(i, pieces):
+            x_sb = xpool.tile([P, UNIT_COLS], BF16, name="x_sb")
+            xt.append(x_sb)
             c0 = unit_pos[i] * UNIT_COLS
             w = UNIT_COLS // pieces
             for s in range(pieces):
                 nc.sync.dma_start(
-                    out=xt[i][:, s * w : (s + 1) * w],
+                    out=x_sb[:, s * w : (s + 1) * w],
                     in_=x_views[unit_group[i]][:, c0 + s * w : c0 + (s + 1) * w],
                 )
 
-        load_x(0, SLOTS)
         for j in range(SLOTS):
             nc.sync.dma_start(out=w1raw[:, j * FEAT : (j + 1) * FEAT], in_=w1v[:, j * FEAT : (j + 1) * FEAT])
-        for i in range(1, UNITS):
+        load_x(0, SLOTS)
+        load_x(1, 2)
+        for i in range(2, UNITS):
             load_x(i, 1)
             if i == SMALL_LOADS_AFTER:
                 nc.sync.dma_start(out=w2raw[:], in_=W2g)
@@ -133,51 +100,79 @@ def tile_gcn_pa_t_kernel(tc, x, W1g, b1g, W2g, b2g, out):
         b1f = const.tile([P, SLOTS], F32)
         b2f = const.tile([P, OUTF], F32)
 
+        permuted = {}
         grouped = {}
         quantised = {}
         accs = {}
-        hidden_parts = {}
+        hidden_sums = {}
         hidden_codes = {}
+        selectors = {}
 
-        def transposes(src_f32, s):
-            bank = tpool.tile([P, 512], F32, name="bank")
-            for v in range(4):
-                nc.tensor.transpose(
-                    bank[:, v * P : (v + 1) * P],
-                    src_f32[:, s * 512 + (v // 2) * 256 + v % 2 : s * 512 + (v // 2 + 1) * 256 : 2],
-                    ident[:],
+        def regroup_x(i, n):
+            perm = ppool.tile([P, UNIT_COLS // 2], F32, name="perm")
+            permuted[i] = perm
+            d = perm[:].rearrange("p (u w) -> p u w", u=2)
+            src = xt[i][:].bitcast(F32)
+            for s0 in range(0, SLOTS, n):
+                nc.vector.tensor_copy(
+                    out=d[:, :, s0 * 256 : (s0 + n) * 256],
+                    in_=src[:, s0 * 512 : (s0 + n) * 512].rearrange("p (w u) -> p u w", u=2),
                 )
+
+        def slot_words(i, s, g, u):
+            if i in permuted:
+                w = u * 1024 + s * 256 + g * P
+                return permuted[i][:, w : w + P]
+            w = s * 512 + g * 256
+            return xt[i][:].bitcast(F32)[:, w + u : w + 256 : 2]
+
+        def transpose_slot(i, s):
+            bank = tpool.tile([P, 512], F32, name="bank")
+            for g in range(2):
+                for u in range(2):
+                    v = g * 2 + u
+                    nc.tensor.transpose(bank[:, v * P : (v + 1) * P], slot_words(i, s, g, u), ident[:])
             return bank
 
-        def copy_slot(slot, bank):
-            i, s = divmod(slot, SLOTS)
+        def copy_slot(i, s, bank):
             if s == 0:
                 grp = gpool.tile([P, UNIT_COLS], BF16, name="grp", align_bytes=64)
                 grouped[i] = grp
-            dst = grouped[i][:].bitcast(F32).rearrange("p (g h q u) -> p g h q u", g=2, h=SLOTS, q=P, u=2)
-            src = bank[:].rearrange("p (g u q) -> p g q u", g=2, u=2, q=P)
-            if slot < VECTOR_HEAD_SLOTS and slot % 2 == 1:
-                nc.vector.tensor_copy(out=dst[:, :, s, :, :], in_=src)
-            else:
-                nc.scalar.copy(out=dst[:, :, s, :, :], in_=src)
+            dst = grouped[i][:].bitcast(F32)[:, s * 512 : (s + 1) * 512]
+            nc.scalar.copy(
+                out=dst.rearrange("p (g q u) -> p g q u", g=2, u=2),
+                in_=bank[:].rearrange("p (g u q) -> p g q u", g=2, u=2),
+            )
 
-        def quant_x(i):
+        def quant_x(i, n):
             codes = cpool.tile([P, UNIT_WORDS], U32, name="codes", align_bytes=64)
             scales = cpool.tile([P, UNIT_WORDS], U8, name="scales", align_bytes=64)
-            nc.vector.quantize_mx(out=codes[:].bitcast(FP8X4), scales=scales[:], in_=grouped[i][:])
+            for w in range(0, UNIT_WORDS, n * 256):
+                nc.vector.quantize_mx(
+                    out=codes[:, w : w + n * 256].bitcast(FP8X4),
+                    scales=scales[:, w : w + n * 256],
+                    in_=grouped[i][:, 4 * w : 4 * (w + n * 256)],
+                )
             quantised[i] = (codes, scales)
 
         def prep_w1():
-            src = w1raw[:].bitcast(F32)
-            grp_v = w1grp[:].bitcast(F32).rearrange("p (j g m u) -> p j g m u", j=SLOTS, g=2, m=P, u=2)
+            grp_v = w1grp[:].bitcast(F32).rearrange("p (g j m u) -> p g j m u", j=SLOTS, g=2, m=P, u=2)
+            words = w1raw[:].bitcast(F32)
             for j in range(SLOTS):
-                bank = transposes(src, j)
-                nc.scalar.copy(out=grp_v[:, j, :, :, :], in_=bank[:].rearrange("p (g u m) -> p g m u", g=2, u=2, m=P))
-                nc.vector.quantize_mx(
-                    out=w1codes[:, j * 256 : (j + 1) * 256].bitcast(FP8X4),
-                    scales=w1scales[:, j * 256 : (j + 1) * 256],
-                    in_=w1grp[:, j * FEAT : (j + 1) * FEAT],
-                )
+                bank = tpool.tile([P, 512], F32, name="bank")
+                for g in range(2):
+                    for u in range(2):
+                        v = g * 2 + u
+                        w = j * 512 + g * 256
+                        nc.tensor.transpose(bank[:, v * P : (v + 1) * P], words[:, w + u : w + 256 : 2], ident[:])
+                nc.scalar.copy(out=grp_v[:, :, j, :, :], in_=bank[:].rearrange("p (g u m) -> p g m u", g=2, u=2, m=P))
+                for g in range(2):
+                    w = (g * SLOTS + j) * P
+                    nc.vector.quantize_mx(
+                        out=w1codes[:, w : w + P].bitcast(FP8X4),
+                        scales=w1scales[:, w : w + P],
+                        in_=w1grp[:, 4 * w : 4 * (w + P)],
+                    )
 
         def prep_small():
             src = w2raw[:].bitcast(F32).rearrange("p (w u) -> p u w", u=2)
@@ -191,57 +186,69 @@ def tile_gcn_pa_t_kernel(tc, x, W1g, b1g, W2g, b2g, out):
             nc.vector.tensor_copy(out=b1f[:], in_=b1raw[:])
             nc.vector.tensor_copy(out=b2f[:], in_=b2raw[:])
             nc.vector.quantize_mx(out=w2codes[:].bitcast(FP8X4), scales=w2scales[:], in_=w2grp[:])
+            for n_units in GROUP_UNITS:
+                if n_units not in selectors:
+                    nb = 8 * n_units
+                    sel = const.tile([P, nb], F32, name="sel%d" % n_units)
+                    nc.vector.tensor_reduce(
+                        out=sel[:], in_=ident[:].rearrange("p (b r) -> p b r", b=nb), axis=AX.X, op=ALU.add
+                    )
+                    selectors[n_units] = sel
 
-        def one_pass(grp_i, i, j, g):
-            first = unit_pos[i] == 0 and g == 0
-            last = unit_pos[i] == GROUP_UNITS[grp_i] - 1 and g == 1
-            if first:
-                acc = apool.tile([P, 512], F32, name="acc%d" % j)
-                accs[j] = acc
+        def passes(i):
+            grp_i = unit_group[i]
             codes, scales = quantised[i]
-            w = (j * 2 + g) * P
-            parts = 2 if grp_i in NARROW_GROUPS else 1
-            width = 512 // parts
-            for part in range(parts):
-                c0 = g * 512 + part * width
-                nc.tensor.matmul_mx(
-                    out=accs[j][:, 0:width],
-                    lhsT=w1codes[:, w : w + P].bitcast(FP8X4),
-                    lhsT_scale=w1scales[:, w : w + P],
-                    rhs=codes[:, c0 : c0 + width].bitcast(FP8X4),
-                    rhs_scale=scales[:, c0 : c0 + width],
-                    start=(first and part == 0),
-                    stop=(last and part == parts - 1),
-                )
-            return last
+            if unit_pos[i] == 0:
+                acc = apool.tile([P, HID], F32, name="acc")
+                accs[grp_i] = acc
+            for s in range(SLOTS):
+                for g in range(2):
+                    w = (s * 2 + g) * P
+                    nc.tensor.matmul_mx(
+                        out=accs[grp_i][:],
+                        lhsT=codes[:, w : w + P].bitcast(FP8X4),
+                        lhsT_scale=scales[:, w : w + P],
+                        rhs=w1codes[:, g * HID : (g + 1) * HID].bitcast(FP8X4),
+                        rhs_scale=w1scales[:, g * HID : (g + 1) * HID],
+                        start=(unit_pos[i] == 0 and s == 0 and g == 0),
+                        stop=(unit_pos[i] == GROUP_UNITS[grp_i] - 1 and s == SLOTS - 1 and g == 1),
+                    )
 
-        def node_sum(grp_i, j):
+        def close_group(grp_i):
+            sums = epool.tile([P, HID], F32, name="sums")
+            nc.scalar.copy(out=sums[:], in_=accs[grp_i][:])
+            hidden_sums[grp_i] = sums
+
+        def hidden(grp_i):
             nb = 8 * GROUP_UNITS[grp_i]
-            parts = 2 if grp_i in NARROW_GROUPS else 1
-            if j == 0:
-                sums = epool.tile([P, 256], F32, name="sums")
-                m1pre = epool.tile([P, HID], BF16, name="m1pre")
-                hidden_parts[grp_i] = (sums, m1pre)
-            sums, m1pre = hidden_parts[grp_i]
-            nc.vector.tensor_reduce(
-                out=sums[:, j * nb : (j + 1) * nb],
-                in_=accs[j][:, 0 : 512 // parts].rearrange("p (h b l) -> p b h l", h=SLOTS // parts, b=nb, l=P // nb),
-                axis=AX.XY,
-                op=ALU.add,
-            )
-            nc.vector.tensor_scalar(
-                out=m1pre[:].rearrange("p (b r j) -> p b r j", b=nb, r=P // nb, j=SLOTS)[:, :, :, j],
-                in0=sums[:, j * nb : (j + 1) * nb].unsqueeze(2).to_broadcast([P, nb, P // nb]),
-                scalar1=1.0 / NODES,
-                scalar2=b1f[:, j : j + 1],
+            sums = hidden_sums[grp_i]
+            bank = tpool.tile([P, 512], F32, name="bank")
+            for j in range(SLOTS):
+                nc.tensor.matmul(
+                    out=bank[:, j * nb : (j + 1) * nb],
+                    lhsT=sums[:, j * P : (j + 1) * P],
+                    rhs=selectors[GROUP_UNITS[grp_i]][:],
+                    start=True,
+                    stop=True,
+                )
+            m1pre = epool.tile([P, 256], F32, name="m1pre")
+            nc.vector.scalar_tensor_tensor(
+                out=m1pre[:, 0 : 4 * nb].rearrange("p (b j) -> p b j", j=SLOTS),
+                in0=bank[:, 0 : 4 * nb].rearrange("p (j b) -> p b j", j=SLOTS),
+                scalar=1.0 / NODES,
+                in1=b1f[:].unsqueeze(1).to_broadcast([P, nb, SLOTS]),
                 op0=ALU.mult,
                 op1=ALU.add,
             )
-
-        def hidden(grp_i):
-            m1pre = hidden_parts[grp_i][1]
             m1 = epool.tile([P, HID], BF16, name="m1", align_bytes=64)
-            nc.vector.tensor_scalar_max(out=m1[:], in0=m1pre[:], scalar1=0.0)
+            nc.vector.tensor_scalar_max(
+                out=m1[:].rearrange("p (b r j) -> p b r j", b=nb, j=SLOTS),
+                in0=m1pre[:, 0 : 4 * nb]
+                .rearrange("p (b j) -> p b j", j=SLOTS)
+                .unsqueeze(2)
+                .to_broadcast([P, nb, P // nb, SLOTS]),
+                scalar1=0.0,
+            )
             m1codes = epool.tile([P, P], U32, name="m1codes", align_bytes=64)
             m1scales = epool.tile([P, P], U8, name="m1scales", align_bytes=64)
             nc.vector.quantize_mx(out=m1codes[:].bitcast(FP8X4), scales=m1scales[:], in_=m1[:])
@@ -266,47 +273,41 @@ def tile_gcn_pa_t_kernel(tc, x, W1g, b1g, W2g, b2g, out):
             n_rep = SLOTS * GROUP_UNITS[grp_i]
             nc.sync.dma_start(out=o_views[grp_i], in_=m2[:].unsqueeze(1).to_broadcast([P, n_rep, OUTF]))
 
-        pass_order = plan_passes()
-        n_slots = 0
-        n_passes = 0
-        n_quant = 0
-        to_hide = []
-        to_second = []
-        for step, (run_slots, run_passes) in enumerate(plan_steps()):
-            while n_quant < UNITS and SLOTS * (n_quant + 1) <= n_slots:
-                quant_x(n_quant)
-                n_quant += 1
-            for grp_i in to_hide:
-                hidden(grp_i)
-            to_hide = []
+        def transpose_unit(i):
             banks = []
-            for k in range(run_slots):
-                i, s = divmod(n_slots + k, SLOTS)
-                banks.append(transposes(xt[i][:].bitcast(F32), s))
-            for k in range(run_slots):
-                copy_slot(n_slots + k, banks[k])
-            n_slots += run_slots
-            if step == 0:
-                quant_x(0)
-                n_quant = 1
-                prep_w1()
-            if step == SMALL_STEP:
+            for s in range(SLOTS):
+                banks.append(transpose_slot(i, s))
+            for s in range(SLOTS):
+                copy_slot(i, s, banks[s])
+
+        prep_w1()
+        transpose_unit(0)
+        quant_x(0, 1)
+        regroup_x(1, 2)
+        passes(0)
+        transpose_unit(1)
+        regroup_x(2, 4)
+        quant_x(1, 2)
+        regroup_x(3, 4)
+        closing = []
+        for i in range(1, UNITS):
+            if i + 1 < UNITS:
+                transpose_unit(i + 1)
+            if i == SMALL_STEP:
                 prep_small()
-            for k in range(run_passes):
-                grp_i, i, j, g = pass_order[n_passes]
-                closes = one_pass(grp_i, i, j, g)
-                n_passes += 1
-                if closes:
-                    node_sum(grp_i, j)
-                    if j == SLOTS - 1:
-                        to_hide.append(grp_i)
-                        to_second.append((grp_i, n_passes))
-            if n_passes == UNITS * PASSES:
-                for grp_i in to_hide:
-                    hidden(grp_i)
-                to_hide = []
-            while to_second and (
-                n_passes - to_second[0][1] >= SECOND_LAG[to_second[0][0]] or n_passes == UNITS * PASSES
-            ):
-                second(to_second[0][0])
-                to_second = to_second[1:]
+            for grp_i in closing:
+                hidden(grp_i)
+            passes(i)
+            if i + 1 < UNITS:
+                quant_x(i + 1, 2)
+            if i + 3 < UNITS:
+                regroup_x(i + 3, 4)
+            for grp_i in closing:
+                second(grp_i)
+            closing = []
+            if unit_pos[i] == GROUP_UNITS[unit_group[i]] - 1:
+                close_group(unit_group[i])
+                closing = [unit_group[i]]
+        for grp_i in closing:
+            hidden(grp_i)
+            second(grp_i)

@@ -18,6 +18,7 @@ HID = 512
 OUTF = 128
 SLOTS = 4
 UNITS = 16
+HALVES = 2 * UNITS
 UNIT_COLS = SLOTS * FEAT
 UNIT_WORDS = UNIT_COLS // 4
 
@@ -25,7 +26,7 @@ FLOPS = 2 * 8192 * FEAT * HID + 2 * 128 * HID * OUTF
 
 GROUP_UNITS = (8, 4, 2, 2)
 SMALL_LOADS_AFTER = 4
-SMALL_STEP = 3
+SMALL_STEP = 7
 
 
 def tile_gcn_pa_t_kernel(tc, x, W1g, b1g, W2g, b2g, out):
@@ -34,7 +35,7 @@ def tile_gcn_pa_t_kernel(tc, x, W1g, b1g, W2g, b2g, out):
     with ctx:
         const = ctx.enter_context(tc.tile_pool(name="const", bufs=1))
         xpool = ctx.enter_context(tc.tile_pool(name="xpool", bufs=12))
-        ppool = ctx.enter_context(tc.tile_pool(name="ppool", bufs=3))
+        ppool = ctx.enter_context(tc.tile_pool(name="ppool", bufs=5))
         gpool = ctx.enter_context(tc.tile_pool(name="gpool", bufs=3))
         cpool = ctx.enter_context(tc.tile_pool(name="cpool", bufs=4))
         epool = ctx.enter_context(tc.tile_pool(name="epool", bufs=2))
@@ -108,21 +109,20 @@ def tile_gcn_pa_t_kernel(tc, x, W1g, b1g, W2g, b2g, out):
         hidden_codes = {}
         selectors = {}
 
-        def regroup_x(i, n):
-            perm = ppool.tile([P, UNIT_COLS // 2], F32, name="perm")
-            permuted[i] = perm
-            d = perm[:].rearrange("p (u w) -> p u w", u=2)
-            src = xt[i][:].bitcast(F32)
-            for s0 in range(0, SLOTS, n):
-                nc.vector.tensor_copy(
-                    out=d[:, :, s0 * 256 : (s0 + n) * 256],
-                    in_=src[:, s0 * 512 : (s0 + n) * 512].rearrange("p (w u) -> p u w", u=2),
-                )
+        def regroup_half(h):
+            i, s0 = h // 2, 2 * (h % 2)
+            perm = ppool.tile([P, UNIT_COLS // 4], F32, name="perm")
+            permuted[h] = perm
+            nc.vector.tensor_copy(
+                out=perm[:].rearrange("p (u w) -> p u w", u=2),
+                in_=xt[i][:].bitcast(F32)[:, s0 * 512 : (s0 + 2) * 512].rearrange("p (w u) -> p u w", u=2),
+            )
 
         def slot_words(i, s, g, u):
-            if i in permuted:
-                w = u * 1024 + s * 256 + g * P
-                return permuted[i][:, w : w + P]
+            h = 2 * i + s // 2
+            if h in permuted:
+                w = u * 512 + (s % 2) * 256 + g * P
+                return permuted[h][:, w : w + P]
             w = s * 512 + g * 256
             return xt[i][:].bitcast(F32)[:, w + u : w + 256 : 2]
 
@@ -144,16 +144,20 @@ def tile_gcn_pa_t_kernel(tc, x, W1g, b1g, W2g, b2g, out):
                 in_=bank[:].rearrange("p (g u q) -> p g q u", g=2, u=2),
             )
 
-        def quant_x(i, n):
-            codes = cpool.tile([P, UNIT_WORDS], U32, name="codes", align_bytes=64)
-            scales = cpool.tile([P, UNIT_WORDS], U8, name="scales", align_bytes=64)
-            for w in range(0, UNIT_WORDS, n * 256):
+        def quant_half(h, n):
+            i = h // 2
+            if h % 2 == 0:
+                codes = cpool.tile([P, UNIT_WORDS], U32, name="codes", align_bytes=64)
+                scales = cpool.tile([P, UNIT_WORDS], U8, name="scales", align_bytes=64)
+                quantised[i] = (codes, scales)
+            codes, scales = quantised[i]
+            w0 = (h % 2) * 512
+            for w in range(w0, w0 + 512, n * 256):
                 nc.vector.quantize_mx(
                     out=codes[:, w : w + n * 256].bitcast(FP8X4),
                     scales=scales[:, w : w + n * 256],
                     in_=grouped[i][:, 4 * w : 4 * (w + n * 256)],
                 )
-            quantised[i] = (codes, scales)
 
         def prep_w1():
             grp_v = w1grp[:].bitcast(F32).rearrange("p (g j m u) -> p g j m u", j=SLOTS, g=2, m=P, u=2)
@@ -195,13 +199,14 @@ def tile_gcn_pa_t_kernel(tc, x, W1g, b1g, W2g, b2g, out):
                     )
                     selectors[n_units] = sel
 
-        def passes(i):
+        def passes(h):
+            i = h // 2
             grp_i = unit_group[i]
             codes, scales = quantised[i]
-            if unit_pos[i] == 0:
+            if unit_pos[i] == 0 and h % 2 == 0:
                 acc = apool.tile([P, HID], F32, name="acc")
                 accs[grp_i] = acc
-            for s in range(SLOTS):
+            for s in range(2 * (h % 2), 2 * (h % 2) + 2):
                 for g in range(2):
                     w = (s * 2 + g) * P
                     nc.tensor.matmul_mx(
@@ -273,39 +278,46 @@ def tile_gcn_pa_t_kernel(tc, x, W1g, b1g, W2g, b2g, out):
             n_rep = SLOTS * GROUP_UNITS[grp_i]
             nc.sync.dma_start(out=o_views[grp_i], in_=m2[:].unsqueeze(1).to_broadcast([P, n_rep, OUTF]))
 
-        def transpose_unit(i):
+        def transpose_half(h):
+            i, s0 = h // 2, 2 * (h % 2)
             banks = []
-            for s in range(SLOTS):
+            for s in range(s0, s0 + 2):
                 banks.append(transpose_slot(i, s))
-            for s in range(SLOTS):
-                copy_slot(i, s, banks[s])
+            for s in range(s0, s0 + 2):
+                copy_slot(i, s, banks[s - s0])
 
         prep_w1()
-        transpose_unit(0)
-        quant_x(0, 1)
-        regroup_x(1, 2)
+        transpose_half(0)
+        transpose_half(1)
+        quant_half(0, 1)
+        quant_half(1, 1)
+        regroup_half(2)
+        regroup_half(3)
         passes(0)
-        transpose_unit(1)
-        regroup_x(2, 4)
-        quant_x(1, 2)
-        regroup_x(3, 4)
+        transpose_half(2)
+        passes(1)
+        transpose_half(3)
+        regroup_half(4)
+        quant_half(2, 2)
+        regroup_half(5)
         closing = []
-        for i in range(1, UNITS):
-            if i + 1 < UNITS:
-                transpose_unit(i + 1)
-            if i == SMALL_STEP:
+        for h in range(2, HALVES):
+            if h + 2 < HALVES:
+                transpose_half(h + 2)
+            if h == SMALL_STEP:
                 prep_small()
             for grp_i in closing:
                 hidden(grp_i)
-            passes(i)
-            if i + 1 < UNITS:
-                quant_x(i + 1, 2)
-            if i + 3 < UNITS:
-                regroup_x(i + 3, 4)
+            passes(h)
+            if h + 1 < HALVES:
+                quant_half(h + 1, 2)
+            if h + 4 < HALVES:
+                regroup_half(h + 4)
             for grp_i in closing:
                 second(grp_i)
             closing = []
-            if unit_pos[i] == GROUP_UNITS[unit_group[i]] - 1:
+            i = h // 2
+            if h % 2 == 1 and unit_pos[i] == GROUP_UNITS[unit_group[i]] - 1:
                 close_group(unit_group[i])
                 closing = [unit_group[i]]
         for grp_i in closing:

@@ -18,15 +18,31 @@ HID = 512
 OUTF = 128
 SLOTS = 4
 UNITS = 16
-HALVES = 2 * UNITS
+ALL_SLOTS = UNITS * SLOTS
+UNIT_ROWS = SLOTS * P
 UNIT_COLS = SLOTS * FEAT
-UNIT_WORDS = UNIT_COLS // 4
+SLOT_CODES = 256
 
 FLOPS = 2 * 8192 * FEAT * HID + 2 * 128 * HID * OUTF
 
 GROUP_UNITS = (8, 4, 2, 2)
+HEAD_SLOTS = 8
+T_BLOCK = 3
+P_BLOCKS = (3, 2)
+T_LEAD = 2
+R_LEAD = 2
+STAGES = ("turn", "hidden", "second", "finish")
 SMALL_LOADS_AFTER = 4
-SMALL_STEP = 7
+SMALL_STEP = 3
+
+
+def blocks(first, end, sizes):
+    out = []
+    while first < end:
+        n = min(sizes[len(out) % len(sizes)], end - first)
+        out.append(list(range(first, first + n)))
+        first += n
+    return out
 
 
 def tile_gcn_pa_t_kernel(tc, x, W1g, b1g, W2g, b2g, out):
@@ -34,10 +50,10 @@ def tile_gcn_pa_t_kernel(tc, x, W1g, b1g, W2g, b2g, out):
     ctx = ExitStack()
     with ctx:
         const = ctx.enter_context(tc.tile_pool(name="const", bufs=1))
-        xpool = ctx.enter_context(tc.tile_pool(name="xpool", bufs=12))
-        ppool = ctx.enter_context(tc.tile_pool(name="ppool", bufs=5))
-        gpool = ctx.enter_context(tc.tile_pool(name="gpool", bufs=3))
-        cpool = ctx.enter_context(tc.tile_pool(name="cpool", bufs=4))
+        xpool = ctx.enter_context(tc.tile_pool(name="xpool", bufs=14))
+        ppool = ctx.enter_context(tc.tile_pool(name="ppool", bufs=6))
+        gpool = ctx.enter_context(tc.tile_pool(name="gpool", bufs=8))
+        cpool = ctx.enter_context(tc.tile_pool(name="cpool", bufs=16))
         epool = ctx.enter_context(tc.tile_pool(name="epool", bufs=2))
         tpool = ctx.enter_context(tc.psum_pool(name="tpool", bufs=6))
         apool = ctx.enter_context(tc.psum_pool(name="apool", bufs=2))
@@ -51,13 +67,15 @@ def tile_gcn_pa_t_kernel(tc, x, W1g, b1g, W2g, b2g, out):
         o_rows = out.flatten_outer_dims()
         row0 = 0
         for grp_i, n_units in enumerate(GROUP_UNITS):
-            rows = n_units * SLOTS * P
+            rows = n_units * UNIT_ROWS
             x_views.append(x_rows[row0 : row0 + rows, :].rearrange("(q s) f -> q (s f)", q=P))
             o_views.append(o_rows[row0 : row0 + rows, :].rearrange("(q s) o -> q s o", q=P))
             row0 += rows
             for c in range(n_units):
                 unit_group.append(grp_i)
                 unit_pos.append(c)
+        last_group = len(GROUP_UNITS) - 1
+        last_slots = ALL_SLOTS - SLOTS * GROUP_UNITS[last_group]
 
         ident = const.tile([P, P], F32)
         make_identity(nc, ident[:])
@@ -75,26 +93,30 @@ def tile_gcn_pa_t_kernel(tc, x, W1g, b1g, W2g, b2g, out):
             xt.append(x_sb)
             c0 = unit_pos[i] * UNIT_COLS
             w = UNIT_COLS // pieces
-            for s in range(pieces):
+            for k in range(pieces):
                 nc.sync.dma_start(
-                    out=x_sb[:, s * w : (s + 1) * w],
-                    in_=x_views[unit_group[i]][:, c0 + s * w : c0 + (s + 1) * w],
+                    out=x_sb[:, k * w : (k + 1) * w],
+                    in_=x_views[unit_group[i]][:, c0 + k * w : c0 + (k + 1) * w],
                 )
 
         for j in range(SLOTS):
             nc.sync.dma_start(out=w1raw[:, j * FEAT : (j + 1) * FEAT], in_=w1v[:, j * FEAT : (j + 1) * FEAT])
         load_x(0, SLOTS)
         load_x(1, 2)
-        for i in range(2, UNITS):
+        load_x(2, 2)
+        for i in range(3, UNITS):
             load_x(i, 1)
             if i == SMALL_LOADS_AFTER:
                 nc.sync.dma_start(out=w2raw[:], in_=W2g)
                 nc.sync.dma_start(out=b1raw[:], in_=b1g.rearrange("(p j) -> p j", j=SLOTS))
                 nc.sync.dma_start(out=b2raw[:], in_=b2g.partition_broadcast(P))
 
-        w1grp = const.tile([P, UNIT_COLS], BF16, align_bytes=64)
-        w1codes = const.tile([P, UNIT_WORDS], U32, align_bytes=64)
-        w1scales = const.tile([P, UNIT_WORDS], U8, align_bytes=64)
+        w1grp = []
+        for j in range(SLOTS):
+            w1grp_j = const.tile([P, FEAT], BF16, name="w1grp%d" % j, align_bytes=64)
+            w1grp.append(w1grp_j)
+        w1codes = const.tile([P, FEAT], U32, align_bytes=64)
+        w1scales = const.tile([P, FEAT], U8, align_bytes=64)
         w2grp = const.tile([P, HID], BF16, align_bytes=64)
         w2codes = const.tile([P, OUTF], U32, align_bytes=64)
         w2scales = const.tile([P, OUTF], U8, align_bytes=64)
@@ -106,140 +128,159 @@ def tile_gcn_pa_t_kernel(tc, x, W1g, b1g, W2g, b2g, out):
         quantised = {}
         accs = {}
         hidden_sums = {}
+        hidden_banks = {}
+        totals = {}
         hidden_codes = {}
-        selectors = {}
+        out_banks = {}
 
-        def regroup_half(h):
-            i, s0 = h // 2, 2 * (h % 2)
-            perm = ppool.tile([P, UNIT_COLS // 4], F32, name="perm")
-            permuted[h] = perm
+        def raw_words(slot, n):
+            i, s = divmod(slot, SLOTS)
+            return xt[i][:].bitcast(F32)[:, s * 512 : (s + n) * 512]
+
+        def regroup(half):
+            perm = ppool.tile([P, 1024], F32, name="perm")
+            permuted[half] = perm
             nc.vector.tensor_copy(
                 out=perm[:].rearrange("p (u w) -> p u w", u=2),
-                in_=xt[i][:].bitcast(F32)[:, s0 * 512 : (s0 + 2) * 512].rearrange("p (w u) -> p u w", u=2),
+                in_=raw_words(2 * half, 2).rearrange("p (w u) -> p u w", u=2),
             )
 
-        def slot_words(i, s, g, u):
-            h = 2 * i + s // 2
-            if h in permuted:
-                w = u * 512 + (s % 2) * 256 + g * P
-                return permuted[h][:, w : w + P]
-            w = s * 512 + g * 256
-            return xt[i][:].bitcast(F32)[:, w + u : w + 256 : 2]
+        def words_of(slot, g, u):
+            if slot // 2 in permuted:
+                w = u * 512 + (slot % 2) * 256 + g * P
+                return permuted[slot // 2][:, w : w + P]
+            return raw_words(slot, 1)[:, g * 256 + u : (g + 1) * 256 : 2]
 
-        def transpose_slot(i, s):
-            bank = tpool.tile([P, 512], F32, name="bank")
-            for g in range(2):
-                for u in range(2):
-                    v = g * 2 + u
-                    nc.tensor.transpose(bank[:, v * P : (v + 1) * P], slot_words(i, s, g, u), ident[:])
-            return bank
+        def copy_bank(words, bank, engine):
+            dst = words.rearrange("p (g q u) -> p g q u", g=2, u=2)
+            src = bank[:].rearrange("p (g u q) -> p g q u", g=2, u=2)
+            if engine == "vector":
+                nc.vector.tensor_copy(out=dst, in_=src)
+            else:
+                nc.scalar.copy(out=dst, in_=src)
 
-        def copy_slot(i, s, bank):
-            if s == 0:
-                grp = gpool.tile([P, UNIT_COLS], BF16, name="grp", align_bytes=64)
-                grouped[i] = grp
-            dst = grouped[i][:].bitcast(F32)[:, s * 512 : (s + 1) * 512]
-            nc.scalar.copy(
-                out=dst.rearrange("p (g q u) -> p g q u", g=2, u=2),
-                in_=bank[:].rearrange("p (g u q) -> p g q u", g=2, u=2),
-            )
-
-        def quant_half(h, n):
-            i = h // 2
-            if h % 2 == 0:
-                codes = cpool.tile([P, UNIT_WORDS], U32, name="codes", align_bytes=64)
-                scales = cpool.tile([P, UNIT_WORDS], U8, name="scales", align_bytes=64)
-                quantised[i] = (codes, scales)
-            codes, scales = quantised[i]
-            w0 = (h % 2) * 512
-            for w in range(w0, w0 + 512, n * 256):
-                nc.vector.quantize_mx(
-                    out=codes[:, w : w + n * 256].bitcast(FP8X4),
-                    scales=scales[:, w : w + n * 256],
-                    in_=grouped[i][:, 4 * w : 4 * (w + n * 256)],
-                )
-
-        def prep_w1():
-            grp_v = w1grp[:].bitcast(F32).rearrange("p (g j m u) -> p g j m u", j=SLOTS, g=2, m=P, u=2)
-            words = w1raw[:].bitcast(F32)
-            for j in range(SLOTS):
+        def transpose_block(block):
+            banks = []
+            for slot in block:
                 bank = tpool.tile([P, 512], F32, name="bank")
                 for g in range(2):
                     for u in range(2):
                         v = g * 2 + u
-                        w = j * 512 + g * 256
-                        nc.tensor.transpose(bank[:, v * P : (v + 1) * P], words[:, w + u : w + 256 : 2], ident[:])
-                nc.scalar.copy(out=grp_v[:, :, j, :, :], in_=bank[:].rearrange("p (g u m) -> p g m u", g=2, u=2, m=P))
+                        nc.tensor.transpose(bank[:, v * P : (v + 1) * P], words_of(slot, g, u), ident[:])
+                banks.append(bank)
+            for slot, bank in zip(block, banks):
+                grp = gpool.tile([P, FEAT], BF16, name="grp", align_bytes=64)
+                grouped[slot] = grp
+                copy_bank(grp[:].bitcast(F32), bank, "scalar")
+
+        def quant_slot(slot):
+            codes = cpool.tile([P, SLOT_CODES], U32, name="codes", align_bytes=64)
+            scales = cpool.tile([P, SLOT_CODES], U8, name="scales", align_bytes=64)
+            quantised[slot] = (codes, scales)
+            nc.vector.quantize_mx(out=codes[:].bitcast(FP8X4), scales=scales[:], in_=grouped[slot][:])
+
+        def passes(block):
+            for slot in block:
+                i, s = divmod(slot, SLOTS)
+                grp_i = unit_group[i]
+                codes, scales = quantised[slot]
+                first = unit_pos[i] == 0 and s == 0
+                last = unit_pos[i] == GROUP_UNITS[grp_i] - 1 and s == SLOTS - 1
+                if first:
+                    acc = apool.tile([P, HID], F32, name="acc")
+                    accs[grp_i] = acc
                 for g in range(2):
-                    w = (g * SLOTS + j) * P
-                    nc.vector.quantize_mx(
-                        out=w1codes[:, w : w + P].bitcast(FP8X4),
-                        scales=w1scales[:, w : w + P],
-                        in_=w1grp[:, 4 * w : 4 * (w + P)],
+                    nc.tensor.matmul_mx(
+                        out=accs[grp_i][:],
+                        lhsT=codes[:, g * P : (g + 1) * P].bitcast(FP8X4),
+                        lhsT_scale=scales[:, g * P : (g + 1) * P],
+                        rhs=w1codes[:, g * HID : (g + 1) * HID].bitcast(FP8X4),
+                        rhs_scale=w1scales[:, g * HID : (g + 1) * HID],
+                        start=(first and g == 0),
+                        stop=(last and g == 1),
                     )
 
-        def prep_small():
+        def last_passes(j):
+            bank = tpool.tile([P, 512], F32, name="bank")
+            for slot in range(last_slots, ALL_SLOTS):
+                codes, scales = quantised[slot]
+                for g in range(2):
+                    w = g * HID + j * P
+                    nc.tensor.matmul_mx(
+                        out=bank[:, 0:P],
+                        lhsT=w1codes[:, w : w + P].bitcast(FP8X4),
+                        lhsT_scale=w1scales[:, w : w + P],
+                        rhs=codes[:, g * P : (g + 1) * P].bitcast(FP8X4),
+                        rhs_scale=scales[:, g * P : (g + 1) * P],
+                        start=(slot == last_slots and g == 0),
+                        stop=(slot == ALL_SLOTS - 1 and g == 1),
+                    )
+            return bank
+
+        def turn_w1(j, engine):
+            bank = tpool.tile([P, 512], F32, name="bank")
+            words = w1raw[:].bitcast(F32)
+            for g in range(2):
+                for u in range(2):
+                    v = g * 2 + u
+                    w = j * 512 + g * 256
+                    nc.tensor.transpose(bank[:, v * P : (v + 1) * P], words[:, w + u : w + 256 : 2], ident[:])
+            copy_bank(w1grp[j][:].bitcast(F32), bank, engine)
+
+        def quant_w1(j):
+            for g in range(2):
+                w = (g * SLOTS + j) * P
+                nc.vector.quantize_mx(
+                    out=w1codes[:, w : w + P].bitcast(FP8X4),
+                    scales=w1scales[:, w : w + P],
+                    in_=w1grp[j][:, g * 512 : (g + 1) * 512],
+                )
+
+        def turn_w2():
             src = w2raw[:].bitcast(F32).rearrange("p (w u) -> p u w", u=2)
             bank = tpool.tile([P, 512], F32, name="bank")
             for u in range(2):
                 nc.tensor.transpose(bank[:, u * P : (u + 1) * P], src[:, u, :], ident[:])
-            nc.vector.tensor_copy(
+            nc.scalar.copy(
                 out=w2grp[:].bitcast(F32).rearrange("p (o u) -> p o u", u=2),
                 in_=bank[:, 0 : 2 * P].rearrange("p (u o) -> p o u", u=2),
             )
+
+        def quant_w2():
             nc.vector.tensor_copy(out=b1f[:], in_=b1raw[:])
             nc.vector.tensor_copy(out=b2f[:], in_=b2raw[:])
             nc.vector.quantize_mx(out=w2codes[:].bitcast(FP8X4), scales=w2scales[:], in_=w2grp[:])
-            for n_units in GROUP_UNITS:
-                if n_units not in selectors:
-                    nb = 8 * n_units
-                    sel = const.tile([P, nb], F32, name="sel%d" % n_units)
-                    nc.vector.tensor_reduce(
-                        out=sel[:], in_=ident[:].rearrange("p (b r) -> p b r", b=nb), axis=AX.X, op=ALU.add
-                    )
-                    selectors[n_units] = sel
-
-        def passes(h):
-            i = h // 2
-            grp_i = unit_group[i]
-            codes, scales = quantised[i]
-            if unit_pos[i] == 0 and h % 2 == 0:
-                acc = apool.tile([P, HID], F32, name="acc")
-                accs[grp_i] = acc
-            for s in range(2 * (h % 2), 2 * (h % 2) + 2):
-                for g in range(2):
-                    w = (s * 2 + g) * P
-                    nc.tensor.matmul_mx(
-                        out=accs[grp_i][:],
-                        lhsT=codes[:, w : w + P].bitcast(FP8X4),
-                        lhsT_scale=scales[:, w : w + P],
-                        rhs=w1codes[:, g * HID : (g + 1) * HID].bitcast(FP8X4),
-                        rhs_scale=w1scales[:, g * HID : (g + 1) * HID],
-                        start=(unit_pos[i] == 0 and s == 0 and g == 0),
-                        stop=(unit_pos[i] == GROUP_UNITS[grp_i] - 1 and s == SLOTS - 1 and g == 1),
-                    )
 
         def close_group(grp_i):
             sums = epool.tile([P, HID], F32, name="sums")
             nc.scalar.copy(out=sums[:], in_=accs[grp_i][:])
             hidden_sums[grp_i] = sums
 
-        def hidden(grp_i):
-            nb = 8 * GROUP_UNITS[grp_i]
+        def turn_sums(grp_i):
             sums = hidden_sums[grp_i]
             bank = tpool.tile([P, 512], F32, name="bank")
             for j in range(SLOTS):
-                nc.tensor.matmul(
-                    out=bank[:, j * nb : (j + 1) * nb],
-                    lhsT=sums[:, j * P : (j + 1) * P],
-                    rhs=selectors[GROUP_UNITS[grp_i]][:],
-                    start=True,
-                    stop=True,
-                )
+                nc.tensor.transpose(bank[:, j * P : (j + 1) * P], sums[:, j * P : (j + 1) * P], ident[:])
+            hidden_banks[grp_i] = bank
+
+        def add_nodes(grp_i, bank, j, n):
+            nb = 8 * GROUP_UNITS[grp_i]
+            if j == 0:
+                total = epool.tile([P, 256], F32, name="total")
+                totals[grp_i] = total
+            nc.vector.tensor_reduce(
+                out=totals[grp_i][:, j * nb : (j + n) * nb],
+                in_=bank[:, 0 : n * P].rearrange("p (jb r) -> p jb r", r=P // nb),
+                axis=AX.X,
+                op=ALU.add,
+            )
+
+        def quant_hidden(grp_i):
+            nb = 8 * GROUP_UNITS[grp_i]
             m1pre = epool.tile([P, 256], F32, name="m1pre")
             nc.vector.scalar_tensor_tensor(
                 out=m1pre[:, 0 : 4 * nb].rearrange("p (b j) -> p b j", j=SLOTS),
-                in0=bank[:, 0 : 4 * nb].rearrange("p (j b) -> p b j", j=SLOTS),
+                in0=totals[grp_i][:, 0 : 4 * nb].rearrange("p (j b) -> p b j", j=SLOTS),
                 scalar=1.0 / NODES,
                 in1=b1f[:].unsqueeze(1).to_broadcast([P, nb, SLOTS]),
                 op0=ALU.mult,
@@ -259,6 +300,10 @@ def tile_gcn_pa_t_kernel(tc, x, W1g, b1g, W2g, b2g, out):
             nc.vector.quantize_mx(out=m1codes[:].bitcast(FP8X4), scales=m1scales[:], in_=m1[:])
             hidden_codes[grp_i] = (m1codes, m1scales)
 
+        def hidden(grp_i):
+            add_nodes(grp_i, hidden_banks[grp_i], 0, SLOTS)
+            quant_hidden(grp_i)
+
         def second(grp_i):
             m1codes, m1scales = hidden_codes[grp_i]
             bank = tpool.tile([P, 512], F32, name="bank")
@@ -271,6 +316,10 @@ def tile_gcn_pa_t_kernel(tc, x, W1g, b1g, W2g, b2g, out):
                 start=True,
                 stop=True,
             )
+            out_banks[grp_i] = bank
+
+        def finish(grp_i):
+            bank = out_banks[grp_i]
             pre2 = epool.tile([P, OUTF], F32, name="pre2")
             nc.vector.tensor_tensor(out=pre2[:], in0=bank[:, 0:OUTF], in1=b2f[:], op=ALU.add)
             m2 = epool.tile([P, OUTF], F32, name="m2")
@@ -278,48 +327,79 @@ def tile_gcn_pa_t_kernel(tc, x, W1g, b1g, W2g, b2g, out):
             n_rep = SLOTS * GROUP_UNITS[grp_i]
             nc.sync.dma_start(out=o_views[grp_i], in_=m2[:].unsqueeze(1).to_broadcast([P, n_rep, OUTF]))
 
-        def transpose_half(h):
-            i, s0 = h // 2, 2 * (h % 2)
-            banks = []
-            for s in range(s0, s0 + 2):
-                banks.append(transpose_slot(i, s))
-            for s in range(s0, s0 + 2):
-                copy_slot(i, s, banks[s - s0])
+        for j in range(SLOTS):
+            turn_w1(j, "scalar" if j % 2 == 0 else "vector")
+            if j > 1:
+                quant_w1(j - 2)
+        for slot in range(4):
+            transpose_block([slot])
+        quant_w1(2)
+        quant_w1(3)
+        quant_slot(0)
+        quant_slot(1)
+        regroup(2)
+        quant_slot(2)
+        quant_slot(3)
+        regroup(3)
+        passes([0, 1])
+        transpose_block([4, 5])
+        passes([2, 3])
+        transpose_block([6, 7])
+        regroup(4)
+        quant_slot(4)
+        quant_slot(5)
+        regroup(5)
 
-        prep_w1()
-        transpose_half(0)
-        transpose_half(1)
-        quant_half(0, 1)
-        quant_half(1, 1)
-        regroup_half(2)
-        regroup_half(3)
-        passes(0)
-        transpose_half(2)
-        passes(1)
-        transpose_half(3)
-        regroup_half(4)
-        quant_half(2, 2)
-        regroup_half(5)
-        closing = []
-        for h in range(2, HALVES):
-            if h + 2 < HALVES:
-                transpose_half(h + 2)
-            if h == SMALL_STEP:
-                prep_small()
-            for grp_i in closing:
-                hidden(grp_i)
-            passes(h)
-            if h + 1 < HALVES:
-                quant_half(h + 1, 2)
-            if h + 4 < HALVES:
-                regroup_half(h + 4)
-            for grp_i in closing:
-                second(grp_i)
-            closing = []
-            i = h // 2
-            if h % 2 == 1 and unit_pos[i] == GROUP_UNITS[unit_group[i]] - 1:
-                close_group(unit_group[i])
-                closing = [unit_group[i]]
-        for grp_i in closing:
-            hidden(grp_i)
-            second(grp_i)
+        t_blocks = [[4, 5], [6, 7]] + blocks(HEAD_SLOTS, ALL_SLOTS, (T_BLOCK,))
+        p_blocks = [[4, 5], [6, 7]] + blocks(HEAD_SLOTS, last_slots, P_BLOCKS)
+        n_regrouped = 6
+        n_quantised = 6
+        todo = {}
+        ends = {"turn": turn_sums, "hidden": hidden, "second": second, "finish": finish}
+
+        def group_end(k, stage):
+            if (k, stage) in todo:
+                ends[stage](todo[(k, stage)])
+
+        for k, block in enumerate(p_blocks):
+            if k + T_LEAD < len(t_blocks):
+                transpose_block(t_blocks[k + T_LEAD])
+            if k == SMALL_STEP:
+                turn_w2()
+            group_end(k, "turn")
+            passes(block)
+            group_end(k, "second")
+            ready = t_blocks[min(k + T_LEAD - 1, len(t_blocks) - 1)][-1]
+            while n_quantised <= ready:
+                quant_slot(n_quantised)
+                n_quantised += 1
+            soon = t_blocks[min(k + T_LEAD + R_LEAD, len(t_blocks) - 1)][-1]
+            while n_regrouped <= soon // 2:
+                regroup(n_regrouped)
+                n_regrouped += 1
+            if k == SMALL_STEP + 1:
+                quant_w2()
+            group_end(k, "hidden")
+            group_end(k, "finish")
+            for slot in block:
+                i, s = divmod(slot, SLOTS)
+                grp_i = unit_group[i]
+                if s == SLOTS - 1 and unit_pos[i] == GROUP_UNITS[grp_i] - 1:
+                    close_group(grp_i)
+                    for n, stage in enumerate(STAGES):
+                        todo[(k + 2 + n, stage)] = grp_i
+        k = len(p_blocks)
+        for j in range(SLOTS):
+            while n_quantised < ALL_SLOTS:
+                quant_slot(n_quantised)
+                n_quantised += 1
+            bank = last_passes(j)
+            for stage in STAGES:
+                group_end(k + j, stage)
+            add_nodes(last_group, bank, j, 1)
+        for stage in STAGES:
+            for n in range(SLOTS, SLOTS + 3):
+                group_end(k + n, stage)
+        quant_hidden(last_group)
+        second(last_group)
+        finish(last_group)

@@ -27,8 +27,8 @@ FLOPS = 2 * 8192 * FEAT * HID + 2 * 128 * HID * OUTF
 
 GROUP_UNITS = (8, 4, 2, 2)
 HEAD_SLOTS = 8
-T_BLOCK = 3
-P_BLOCKS = (3, 2)
+T_BLOCK = 2
+P_BLOCKS = (2, 2, 2, 1)
 T_LEAD = 2
 R_LEAD = 2
 STAGES = ("turn", "hidden", "second", "finish")

from contextlib import ExitStack

import concourse.mybir as mybir
from concourse.masks import make_identity

F32 = mybir.dt.float32
BF16 = mybir.dt.bfloat16
U32 = mybir.dt.uint32
U8 = mybir.dt.uint8
FP8X4 = mybir.dt.float8_e4m3fn_x4
ALU = mybir.AluOpType
AX = mybir.AxisListType

P = 128
NODES = 64
FEAT = 1024
HID = 512
OUTF = 128
SLOTS = 4
UNITS = 16
ALL_SLOTS = UNITS * SLOTS
UNIT_ROWS = SLOTS * P
UNIT_COLS = SLOTS * FEAT
SLOT_CODES = 256

FLOPS = 2 * 8192 * FEAT * HID + 2 * 128 * HID * OUTF

GROUP_UNITS = (8, 4, 2, 2)
HEAD_SLOTS = 8
T_BLOCK = 2
P_BLOCKS = (2, 2, 2, 1)
T_LEAD = 2
R_LEAD = 2
STAGES = ("turn", "hidden", "second", "finish")
SMALL_LOADS_AFTER = 4
SMALL_STEP = 3


def blocks(first, end, sizes):
    out = []
    while first < end:
        n = min(sizes[len(out) % len(sizes)], end - first)
        out.append(list(range(first, first + n)))
        first += n
    return out


def tile_gcn_pa_t_kernel(tc, x, W1g, b1g, W2g, b2g, out):
    nc = tc.nc
    ctx = ExitStack()
    with ctx:
        const = ctx.enter_context(tc.tile_pool(name="const", bufs=1))
        xpool = ctx.enter_context(tc.tile_pool(name="xpool", bufs=14))
        ppool = ctx.enter_context(tc.tile_pool(name="ppool", bufs=6))
        gpool = ctx.enter_context(tc.tile_pool(name="gpool", bufs=8))
        cpool = ctx.enter_context(tc.tile_pool(name="cpool", bufs=16))
        epool = ctx.enter_context(tc.tile_pool(name="epool", bufs=2))
        tpool = ctx.enter_context(tc.psum_pool(name="tpool", bufs=6))
        apool = ctx.enter_context(tc.psum_pool(name="apool", bufs=2))
        ctx.enter_context(tc.manual_schedule())

        unit_group = []
        unit_pos = []
        x_views = []
        o_views = []
        x_rows = x.flatten_outer_dims()
        o_rows = out.flatten_outer_dims()
        row0 = 0
        for grp_i, n_units in enumerate(GROUP_UNITS):
            rows = n_units * UNIT_ROWS
            x_views.append(x_rows[row0 : row0 + rows, :].rearrange("(q s) f -> q (s f)", q=P))
            o_views.append(o_rows[row0 : row0 + rows, :].rearrange("(q s) o -> q s o", q=P))
            row0 += rows
            for c in range(n_units):
                unit_group.append(grp_i)
                unit_pos.append(c)
        last_group = len(GROUP_UNITS) - 1
        last_slots = ALL_SLOTS - SLOTS * GROUP_UNITS[last_group]

        ident = const.tile([P, P], F32)
        make_identity(nc, ident[:])

        w1raw = const.tile([P, UNIT_COLS], BF16)
        w1v = W1g.rearrange("(p j) k -> p (j k)", j=SLOTS)
        w2raw = const.tile([P, HID], BF16)
        b1raw = const.tile([P, SLOTS], BF16)
        b2raw = const.tile([P, OUTF], BF16)

        xt = []

        def load_x(i, pieces):
            x_sb = xpool.tile([P, UNIT_COLS], BF16, name="x_sb")
            xt.append(x_sb)
            c0 = unit_pos[i] * UNIT_COLS
            w = UNIT_COLS // pieces
            for k in range(pieces):
                nc.sync.dma_start(
                    out=x_sb[:, k * w : (k + 1) * w],
                    in_=x_views[unit_group[i]][:, c0 + k * w : c0 + (k + 1) * w],
                )

        for j in range(SLOTS):
            nc.sync.dma_start(out=w1raw[:, j * FEAT : (j + 1) * FEAT], in_=w1v[:, j * FEAT : (j + 1) * FEAT])
        load_x(0, SLOTS)
        load_x(1, 2)
        load_x(2, 2)
        for i in range(3, UNITS):
            load_x(i, 1)
            if i == SMALL_LOADS_AFTER:
                nc.sync.dma_start(out=w2raw[:], in_=W2g)
                nc.sync.dma_start(out=b1raw[:], in_=b1g.rearrange("(p j) -> p j", j=SLOTS))
                nc.sync.dma_start(out=b2raw[:], in_=b2g.partition_broadcast(P))

        w1grp = []
        for j in range(SLOTS):
            w1grp_j = const.tile([P, FEAT], BF16, name="w1grp%d" % j, align_bytes=64)
            w1grp.append(w1grp_j)
        w1codes = const.tile([P, FEAT], U32, align_bytes=64)
        w1scales = const.tile([P, FEAT], U8, align_bytes=64)
        w2grp = const.tile([P, HID], BF16, align_bytes=64)
        w2codes = const.tile([P, OUTF], U32, align_bytes=64)
        w2scales = const.tile([P, OUTF], U8, align_bytes=64)
        b1f = const.tile([P, SLOTS], F32)
        b2f = const.tile([P, OUTF], F32)

        permuted = {}
        grouped = {}
        quantised = {}
        accs = {}
        hidden_sums = {}
        hidden_banks = {}
        totals = {}
        hidden_codes = {}
        out_banks = {}

        def raw_words(slot, n):
            i, s = divmod(slot, SLOTS)
            return xt[i][:].bitcast(F32)[:, s * 512 : (s + n) * 512]

        def regroup(half):
            perm = ppool.tile([P, 1024], F32, name="perm")
            permuted[half] = perm
            nc.vector.tensor_copy(
                out=perm[:].rearrange("p (u w) -> p u w", u=2),
                in_=raw_words(2 * half, 2).rearrange("p (w u) -> p u w", u=2),
            )

        def words_of(slot, g, u):
            if slot // 2 in permuted:
                w = u * 512 + (slot % 2) * 256 + g * P
                return permuted[slot // 2][:, w : w + P]
            return raw_words(slot, 1)[:, g * 256 + u : (g + 1) * 256 : 2]

        def copy_bank(words, bank, engine):
            dst = words.rearrange("p (g q u) -> p g q u", g=2, u=2)
            src = bank[:].rearrange("p (g u q) -> p g q u", g=2, u=2)
            if engine == "vector":
                nc.vector.tensor_copy(out=dst, in_=src)
            else:
                nc.scalar.copy(out=dst, in_=src)

        def transpose_block(block):
            banks = []
            for slot in block:
                bank = tpool.tile([P, 512], F32, name="bank")
                for g in range(2):
                    for u in range(2):
                        v = g * 2 + u
                        nc.tensor.transpose(bank[:, v * P : (v + 1) * P], words_of(slot, g, u), ident[:])
                banks.append(bank)
            for slot, bank in zip(block, banks):
                grp = gpool.tile([P, FEAT], BF16, name="grp", align_bytes=64)
                grouped[slot] = grp
                copy_bank(grp[:].bitcast(F32), bank, "scalar")

        def quant_slot(slot):
            codes = cpool.tile([P, SLOT_CODES], U32, name="codes", align_bytes=64)
            scales = cpool.tile([P, SLOT_CODES], U8, name="scales", align_bytes=64)
            quantised[slot] = (codes, scales)
            nc.vector.quantize_mx(out=codes[:].bitcast(FP8X4), scales=scales[:], in_=grouped[slot][:])

        def passes(block):
            for slot in block:
                i, s = divmod(slot, SLOTS)
                grp_i = unit_group[i]
                codes, scales = quantised[slot]
                first = unit_pos[i] == 0 and s == 0
                last = unit_pos[i] == GROUP_UNITS[grp_i] - 1 and s == SLOTS - 1
                if first:
                    acc = apool.tile([P, HID], F32, name="acc")
                    accs[grp_i] = acc
                for g in range(2):
                    nc.tensor.matmul_mx(
                        out=accs[grp_i][:],
                        lhsT=codes[:, g * P : (g + 1) * P].bitcast(FP8X4),
                        lhsT_scale=scales[:, g * P : (g + 1) * P],
                        rhs=w1codes[:, g * HID : (g + 1) * HID].bitcast(FP8X4),
                        rhs_scale=w1scales[:, g * HID : (g + 1) * HID],
                        start=(first and g == 0),
                        stop=(last and g == 1),
                    )

        def last_passes(j):
            bank = tpool.tile([P, 512], F32, name="bank")
            for slot in range(last_slots, ALL_SLOTS):
                codes, scales = quantised[slot]
                for g in range(2):
                    w = g * HID + j * P
                    nc.tensor.matmul_mx(
                        out=bank[:, 0:P],
                        lhsT=w1codes[:, w : w + P].bitcast(FP8X4),
                        lhsT_scale=w1scales[:, w : w + P],
                        rhs=codes[:, g * P : (g + 1) * P].bitcast(FP8X4),
                        rhs_scale=scales[:, g * P : (g + 1) * P],
                        start=(slot == last_slots and g == 0),
                        stop=(slot == ALL_SLOTS - 1 and g == 1),
                    )
            return bank

        def turn_w1(j, engine):
            bank = tpool.tile([P, 512], F32, name="bank")
            words = w1raw[:].bitcast(F32)
            for g in range(2):
                for u in range(2):
                    v = g * 2 + u
                    w = j * 512 + g * 256
                    nc.tensor.transpose(bank[:, v * P : (v + 1) * P], words[:, w + u : w + 256 : 2], ident[:])
            copy_bank(w1grp[j][:].bitcast(F32), bank, engine)

        def quant_w1(j):
            for g in range(2):
                w = (g * SLOTS + j) * P
                nc.vector.quantize_mx(
                    out=w1codes[:, w : w + P].bitcast(FP8X4),
                    scales=w1scales[:, w : w + P],
                    in_=w1grp[j][:, g * 512 : (g + 1) * 512],
                )

        def turn_w2():
            src = w2raw[:].bitcast(F32).rearrange("p (w u) -> p u w", u=2)
            bank = tpool.tile([P, 512], F32, name="bank")
            for u in range(2):
                nc.tensor.transpose(bank[:, u * P : (u + 1) * P], src[:, u, :], ident[:])
            nc.scalar.copy(
                out=w2grp[:].bitcast(F32).rearrange("p (o u) -> p o u", u=2),
                in_=bank[:, 0 : 2 * P].rearrange("p (u o) -> p o u", u=2),
            )

        def quant_w2():
            nc.vector.tensor_copy(out=b1f[:], in_=b1raw[:])
            nc.vector.tensor_copy(out=b2f[:], in_=b2raw[:])
            nc.vector.quantize_mx(out=w2codes[:].bitcast(FP8X4), scales=w2scales[:], in_=w2grp[:])

        def close_group(grp_i):
            sums = epool.tile([P, HID], F32, name="sums")
            nc.scalar.copy(out=sums[:], in_=accs[grp_i][:])
            hidden_sums[grp_i] = sums

        def turn_sums(grp_i):
            sums = hidden_sums[grp_i]
            bank = tpool.tile([P, 512], F32, name="bank")
            for j in range(SLOTS):
                nc.tensor.transpose(bank[:, j * P : (j + 1) * P], sums[:, j * P : (j + 1) * P], ident[:])
            hidden_banks[grp_i] = bank

        def add_nodes(grp_i, bank, j, n):
            nb = 8 * GROUP_UNITS[grp_i]
            if j == 0:
                total = epool.tile([P, 256], F32, name="total")
                totals[grp_i] = total
            nc.vector.tensor_reduce(
                out=totals[grp_i][:, j * nb : (j + n) * nb],
                in_=bank[:, 0 : n * P].rearrange("p (jb r) -> p jb r", r=P // nb),
                axis=AX.X,
                op=ALU.add,
            )

        def quant_hidden(grp_i):
            nb = 8 * GROUP_UNITS[grp_i]
            m1pre = epool.tile([P, 256], F32, name="m1pre")
            nc.vector.scalar_tensor_tensor(
                out=m1pre[:, 0 : 4 * nb].rearrange("p (b j) -> p b j", j=SLOTS),
                in0=totals[grp_i][:, 0 : 4 * nb].rearrange("p (j b) -> p b j", j=SLOTS),
                scalar=1.0 / NODES,
                in1=b1f[:].unsqueeze(1).to_broadcast([P, nb, SLOTS]),
                op0=ALU.mult,
                op1=ALU.add,
            )
            m1 = epool.tile([P, HID], BF16, name="m1", align_bytes=64)
            nc.vector.tensor_scalar_max(
                out=m1[:].rearrange("p (b r j) -> p b r j", b=nb, j=SLOTS),
                in0=m1pre[:, 0 : 4 * nb]
                .rearrange("p (b j) -> p b j", j=SLOTS)
                .unsqueeze(2)
                .to_broadcast([P, nb, P // nb, SLOTS]),
                scalar1=0.0,
            )
            m1codes = epool.tile([P, P], U32, name="m1codes", align_bytes=64)
            m1scales = epool.tile([P, P], U8, name="m1scales", align_bytes=64)
            nc.vector.quantize_mx(out=m1codes[:].bitcast(FP8X4), scales=m1scales[:], in_=m1[:])
            hidden_codes[grp_i] = (m1codes, m1scales)

        def hidden(grp_i):
            add_nodes(grp_i, hidden_banks[grp_i], 0, SLOTS)
            quant_hidden(grp_i)

        def second(grp_i):
            m1codes, m1scales = hidden_codes[grp_i]
            bank = tpool.tile([P, 512], F32, name="bank")
            nc.tensor.matmul_mx(
                out=bank[:, 0:OUTF],
                lhsT=m1codes[:].bitcast(FP8X4),
                lhsT_scale=m1scales[:],
                rhs=w2codes[:].bitcast(FP8X4),
                rhs_scale=w2scales[:],
                start=True,
                stop=True,
            )
            out_banks[grp_i] = bank

        def finish(grp_i):
            bank = out_banks[grp_i]
            pre2 = epool.tile([P, OUTF], F32, name="pre2")
            nc.vector.tensor_tensor(out=pre2[:], in0=bank[:, 0:OUTF], in1=b2f[:], op=ALU.add)
            m2 = epool.tile([P, OUTF], F32, name="m2")
            nc.vector.tensor_scalar_max(out=m2[:], in0=pre2[:], scalar1=0.0)
            n_rep = SLOTS * GROUP_UNITS[grp_i]
            nc.sync.dma_start(out=o_views[grp_i], in_=m2[:].unsqueeze(1).to_broadcast([P, n_rep, OUTF]))

        for j in range(SLOTS):
            turn_w1(j, "scalar" if j % 2 == 0 else "vector")
            if j > 1:
                quant_w1(j - 2)
        for slot in range(4):
            transpose_block([slot])
        quant_w1(2)
        quant_w1(3)
        quant_slot(0)
        quant_slot(1)
        regroup(2)
        quant_slot(2)
        quant_slot(3)
        regroup(3)
        passes([0, 1])
        transpose_block([4, 5])
        passes([2, 3])
        transpose_block([6, 7])
        regroup(4)
        quant_slot(4)
        quant_slot(5)
        regroup(5)

        t_blocks = [[4, 5], [6, 7]] + blocks(HEAD_SLOTS, ALL_SLOTS, (T_BLOCK,))
        p_blocks = [[4, 5], [6, 7]] + blocks(HEAD_SLOTS, last_slots, P_BLOCKS)
        n_regrouped = 6
        n_quantised = 6
        todo = {}
        ends = {"turn": turn_sums, "hidden": hidden, "second": second, "finish": finish}

        def group_end(k, stage):
            if (k, stage) in todo:
                ends[stage](todo[(k, stage)])

        for k, block in enumerate(p_blocks):
            if k + T_LEAD < len(t_blocks):
                transpose_block(t_blocks[k + T_LEAD])
            if k == SMALL_STEP:
                turn_w2()
            group_end(k, "turn")
            passes(block)
            group_end(k, "second")
            ready = t_blocks[min(k + T_LEAD - 1, len(t_blocks) - 1)][-1]
            while n_quantised <= ready:
                quant_slot(n_quantised)
                n_quantised += 1
            soon = t_blocks[min(k + T_LEAD + R_LEAD, len(t_blocks) - 1)][-1]
            while n_regrouped <= soon // 2:
                regroup(n_regrouped)
                n_regrouped += 1
            if k == SMALL_STEP + 1:
                quant_w2()
            group_end(k, "hidden")
            group_end(k, "finish")
            for slot in block:
                i, s = divmod(slot, SLOTS)
                grp_i = unit_group[i]
                if s == SLOTS - 1 and unit_pos[i] == GROUP_UNITS[grp_i] - 1:
                    close_group(grp_i)
                    for n, stage in enumerate(STAGES):
                        todo[(k + 2 + n, stage)] = grp_i
        k = len(p_blocks)
        for j in range(SLOTS):
            while n_quantised < ALL_SLOTS:
                quant_slot(n_quantised)
                n_quantised += 1
            bank = last_passes(j)
            for stage in STAGES:
                group_end(k + j, stage)
            add_nodes(last_group, bank, j, 1)
        for stage in STAGES:
            for n in range(SLOTS, SLOTS + 3):
                group_end(k + n, stage)
        quant_hidden(last_group)
        second(last_group)
        finish(last_group)
